import numpy as np
import ml_dtypes


def mxq(x, axis, fmt="e4m3"):
    dtype, down = {"e4m3": (ml_dtypes.float8_e4m3fn, 7), "e5m2": (ml_dtypes.float8_e5m2, 14)}[fmt]
    v = np.moveaxis(np.asarray(x, np.float32).astype(ml_dtypes.bfloat16).astype(np.float64), axis, -1)
    blocks = v.reshape(v.shape[:-1] + (-1, 32))
    amax = np.abs(blocks).max(-1, keepdims=True)
    byte = np.maximum(np.where(amax > 0, np.frexp(amax)[1] - 1 + 127, 0) - down, 1)
    scale = np.exp2(byte - 127.0)
    codes = (blocks / scale).astype(np.float32).astype(dtype).astype(np.float64)
    return np.moveaxis((codes * scale).reshape(v.shape), -1, axis)


WIDE = False


def mx_kscale(k):
    if not WIDE:
        return np.ones(k)
    levels = np.array([10, -10, 5, -5, 0])
    if k % 512:
        return np.exp2(np.random.permutation(np.resize(levels, k // 32))).repeat(32)
    a = np.empty((k // 512, 16))
    for p in range(k // 512):
        a[p, :8] = np.random.permutation(np.resize(levels, 8))
        for g in range(8):
            far = levels[np.abs(levels - a[p, g]) >= 10]
            a[p, g + 8] = far[np.random.randint(len(far))]
    return np.exp2(a.ravel()).repeat(32)


BF16 = ml_dtypes.bfloat16


def bf(x):
    return np.asarray(x, np.float32).astype(BF16)


def f64(x):
    return np.asarray(x).astype(np.float64)


B, N, DIM, HEADS, WIN, FF, TIME_DIM = 1, 1536, 1024, 8, 512, 2048, 512
HD = DIM // HEADS
EPS = 1e-5


def layernorm(x, g, b):
    mu = x.mean(-1, keepdims=True)
    var = np.square(x - mu).mean(-1, keepdims=True)
    return (x - mu) / np.sqrt(var + EPS) * g + b


def setup_inputs():
    s = mx_kscale(DIM)
    return {
        "x": bf(np.random.standard_normal((B, N, DIM)) * (0.5 + 1.5 * np.random.random((B, N, 1))) + 0.5 * np.random.standard_normal((B, N, 1))),
        "t_scale": bf(np.random.standard_normal((B, DIM)) * 0.5),
        "t_shift": bf(np.random.standard_normal((B, DIM)) * 0.5 * s),
        "ln1_g": bf((1.0 + 0.1 * np.random.standard_normal(DIM)) * s),
        "ln1_b": bf(0.1 * np.random.standard_normal(DIM) * s),
        "qkv_w": bf(np.random.standard_normal((DIM, 3 * DIM)) * 1.2 / np.sqrt(DIM) / s[:, None]),
        "qkv_b": bf(np.random.standard_normal(3 * DIM) * 0.2),
    }


def reference(x, t_scale, t_shift, ln1_g, ln1_b, qkv_w, qkv_b):
    x_norm = layernorm(f64(x), f64(ln1_g), f64(ln1_b)) * (1.0 + f64(t_scale)[:, None, :]) + f64(t_shift)[:, None, :]
    qkv = (mxq(x_norm, 2, "e4m3") @ mxq(f64(qkv_w), 0, "e4m3")) + f64(qkv_b)
    return qkv.reshape(B, N, 3, HEADS, HD).transpose(2, 0, 3, 1, 4)

@@ -1,0 +1,220 @@
+from contextlib import ExitStack
+
+import concourse.mybir as mybir
+from concourse.masks import make_identity
+
+F32 = mybir.dt.float32
+BF16 = mybir.dt.bfloat16
+U32 = mybir.dt.uint32
+U8 = mybir.dt.uint8
+FP8X4 = mybir.dt.float8_e4m3fn_x4
+ALU = mybir.AluOpType
+ACT = mybir.ActivationFunctionType
+
+P = 128
+TOKENS = 1536
+DIM = 1024
+COLS = 3072
+HEAD_DIM = 128
+EPS = 1e-5
+
+PACK = 4
+K_PASS = P * PACK
+PASSES = DIM // K_PASS
+K_CHUNKS = DIM // P
+TILES = TOKENS // P
+GROUP_TILES = 4
+GROUPS = TILES // GROUP_TILES
+GROUP_TOKENS = GROUP_TILES * P
+N_COLS = 512
+COL_GROUPS = COLS // N_COLS
+GROUP_HEADS = N_COLS // HEAD_DIM
+LOAD_COLS = 1024
+LOADS = COLS // LOAD_COLS
+BN_WIDTH = 512
+BN_PARTS = DIM // BN_WIDTH
+BN_STATS = 6
+RUN = 4
+
+FLOPS = 2 * TOKENS * DIM * COLS
+
+
+def tile_localattentionblock_pa_kernel(
+    tc, x, t_scale, t_shift, ln1_g, ln1_b, qkv_w, qkv_b, out
+):
+    nc = tc.nc
+
+    x_view = x.rearrange("b (p t) k -> p (b t) k", t=TILES)
+    out_view = out.rearrange("j b h (p t) d -> p (j b h) t d", t=TILES)
+    w_view = qkv_w.rearrange("(g p t) n -> g p t n", t=PACK, p=P)
+
+    with ExitStack() as ctx:
+        keep = ctx.enter_context(tc.tile_pool(name="keep", bufs=1))
+        small = ctx.enter_context(tc.tile_pool(name="small", bufs=2 * GROUP_TILES))
+        xhat_pool = ctx.enter_context(tc.tile_pool(name="xhat_pool", bufs=2 * GROUP_TILES))
+        xn_pool = ctx.enter_context(tc.tile_pool(name="xn_pool", bufs=2))
+        grouped_pool = ctx.enter_context(tc.tile_pool(name="grouped_pool", bufs=4))
+        stage_pool = ctx.enter_context(tc.tile_pool(name="stage_pool", bufs=4))
+        xt_psum = ctx.enter_context(tc.psum_pool(name="xt_psum", bufs=4))
+        acc_psum = ctx.enter_context(tc.psum_pool(name="acc_psum", bufs=4))
+
+        eps = keep.tile([P, 1], F32, name="eps")
+        nc.vector.memset(eps[:], EPS)
+        warm = keep.tile([P, 1], F32, name="warm")
+        nc.scalar.activation(out=warm[:], in_=eps[:], func=ACT.Sqrt)
+        ident = keep.tile([P, P], F32, name="ident")
+        make_identity(nc, ident[:])
+
+        x_sb = [keep.tile([P, DIM], BF16, name="x_sb%d" % t) for t in range(TILES)]
+        w_raw = [
+            [keep.tile([P, PACK, LOAD_COLS], BF16, name="w_raw%d_%d" % (g, l)) for l in range(LOADS)]
+            for g in range(PASSES)
+        ]
+        bias = keep.tile([P, COLS], BF16, name="bias")
+
+        def load_x(group):
+            for t in range(group * GROUP_TILES, (group + 1) * GROUP_TILES):
+                nc.sync.dma_start(out=x_sb[t][:], in_=x_view[:, t, :])
+
+        def load_w(l):
+            for g in range(PASSES):
+                nc.sync.dma_start(
+                    out=w_raw[g][l][:], in_=w_view[g, :, :, l * LOAD_COLS : (l + 1) * LOAD_COLS]
+                )
+
+        vec_rows = keep.tile([P, K_PASS], BF16, name="vec_rows")
+        nc.vector.memset(vec_rows[:], 0.0)
+        vectors = [
+            ln1_g.rearrange("(r c) -> r c", c=K_PASS),
+            ln1_b.rearrange("(r c) -> r c", c=K_PASS),
+            t_scale.rearrange("b (r c) -> (b r) c", c=K_PASS),
+            t_shift.rearrange("b (r c) -> (b r) c", c=K_PASS),
+        ]
+        for v in range(len(vectors)):
+            nc.scalar.dma_start(out=vec_rows[v * PASSES : (v + 1) * PASSES, :], in_=vectors[v])
+        load_x(0)
+        load_w(0)
+        load_x(1)
+        load_x(2)
+        load_w(1)
+        nc.sync.dma_start(out=bias[:], in_=qkv_b.partition_broadcast(P))
+        load_w(2)
+
+        vec_f32 = keep.tile([P, PACK, P], F32, name="vec_f32")
+        nc.vector.tensor_copy(out=vec_f32[:], in_=vec_rows[:].rearrange("r (q t) -> r t q", t=PACK))
+        vec_t = xt_psum.tile([P, GROUP_TOKENS], F32, name="xt")
+        for t in range(PACK):
+            nc.tensor.transpose(vec_t[:, t * P : (t + 1) * P], vec_f32[:, t, :], ident[:])
+        by_row = vec_t[:].rearrange("p (t r) -> p r t", t=PACK)
+        g_rows, b_rows, scale_rows, shift_rows = [by_row[:, v * PASSES : (v + 1) * PASSES, :] for v in range(len(vectors))]
+        one_plus = keep.tile([P, PASSES, PACK], F32, name="one_plus")
+        gain = keep.tile([P, PASSES, PACK], F32, name="gain")
+        shift = keep.tile([P, PASSES, PACK], F32, name="shift")
+        nc.vector.tensor_scalar_add(out=one_plus[:], in0=scale_rows, scalar1=1.0)
+        nc.vector.tensor_tensor(out=gain[:], in0=g_rows, in1=one_plus[:], op=ALU.mult)
+        nc.vector.tensor_tensor(out=shift[:], in0=b_rows, in1=one_plus[:], op=ALU.mult)
+        nc.vector.tensor_tensor(out=shift[:], in0=shift_rows, in1=shift[:], op=ALU.add)
+
+        x_codes = [keep.tile([P, PASSES, GROUP_TOKENS], U32, name="x_codes%d" % g, align_bytes=64) for g in range(GROUPS)]
+        x_scales = [keep.tile([P, PASSES, GROUP_TOKENS], U8, name="x_scales%d" % g, align_bytes=64) for g in range(GROUPS)]
+        w_codes = [keep.tile([P, PASSES, N_COLS], U32, name="w_codes%d" % c, align_bytes=64) for c in range(COL_GROUPS)]
+        w_scales = [keep.tile([P, PASSES, N_COLS], U8, name="w_scales%d" % c, align_bytes=64) for c in range(COL_GROUPS)]
+
+        def regroup(copy, rows):
+            grouped = grouped_pool.tile([P, N_COLS, PACK], BF16, name="grouped", align_bytes=64)
+            copy(
+                out=grouped[:].rearrange("p (c i) t -> p c t i", i=RUN),
+                in_=rows.rearrange("p t (c i) -> p c t i", i=RUN),
+            )
+            return grouped
+
+        def quantise(grouped, codes, scales):
+            nc.vector.quantize_mx(
+                out=codes.bitcast(FP8X4), scales=scales, in_=grouped[:].rearrange("p n t -> p (n t)")
+            )
+
+        def normalise(group):
+            xhat = []
+            for t in range(group * GROUP_TILES, (group + 1) * GROUP_TILES):
+                stats = small.tile([P, BN_PARTS, BN_STATS], F32, name="stats")
+                for h in range(BN_PARTS):
+                    nc.vector.bn_stats(out=stats[:, h, :], in_=x_sb[t][:, h * BN_WIDTH : (h + 1) * BN_WIDTH])
+                mean_var = small.tile([P, 2], F32, name="mean_var")
+                nc.vector.bn_aggr(out=mean_var[:], in_=stats[:].rearrange("p h s -> p (h s)"))
+                neg_mean = small.tile([P, 1], F32, name="neg_mean")
+                nc.scalar.mul(out=neg_mean[:], in_=mean_var[:, 0:1], mul=-1.0)
+                std = small.tile([P, 1], F32, name="std")
+                nc.scalar.activation(out=std[:], in_=mean_var[:, 1:2], func=ACT.Sqrt, bias=eps[:], scale=1.0)
+                rstd = small.tile([P, 1], F32, name="rstd")
+                nc.vector.reciprocal(out=rstd[:], in_=std[:])
+                xhat_t = xhat_pool.tile([P, DIM], F32, name="xhat")
+                nc.gpsimd.tensor_scalar(
+                    out=xhat_t[:].rearrange("p (g t q) -> p g t q", g=PASSES, t=PACK),
+                    in0=x_sb[t][:].rearrange("p (g q t) -> p g t q", g=PASSES, t=PACK),
+                    scalar1=neg_mean[:], scalar2=rstd[:],
+                    op0=ALU.add, op1=ALU.mult,
+                )
+                xhat.append(xhat_t)
+            return xhat
+
+        def quantise_tokens(group, xhat):
+            xn = xn_pool.tile([P, K_CHUNKS, GROUP_TOKENS], BF16, name="xn")
+            for c in range(K_CHUNKS):
+                xt = xt_psum.tile([P, GROUP_TOKENS], F32, name="xt")
+                for i in range(GROUP_TILES):
+                    nc.tensor.transpose(xt[:, i * P : (i + 1) * P], xhat[i][:, c * P : (c + 1) * P], ident[:])
+                nc.scalar.activation(
+                    out=xn[:, c, :], in_=xt[:], func=ACT.Identity, scale=gain[:, c // PACK, c % PACK : c % PACK + 1], bias=shift[:, c // PACK, c % PACK : c % PACK + 1]
+                )
+            grouped = [regroup(nc.vector.tensor_copy, xn[:, g * PACK : (g + 1) * PACK, :]) for g in range(PASSES)]
+            for g in range(PASSES):
+                quantise(grouped[g], x_codes[group][:, g, :], x_scales[group][:, g, :])
+
+        def quantise_columns(c):
+            l = c * N_COLS // LOAD_COLS
+            first = c * N_COLS - l * LOAD_COLS
+            grouped = [regroup(nc.scalar.copy, w_raw[g][l][:, :, first : first + N_COLS]) for g in range(PASSES)]
+            for g in range(PASSES):
+                quantise(grouped[g], w_codes[c][:, g, :], w_scales[c][:, g, :])
+
+        def project(group, c):
+            stage = stage_pool.tile([P, GROUP_HEADS, GROUP_TILES, HEAD_DIM], F32, name="stage")
+            bias_heads = bias[:, c * N_COLS : (c + 1) * N_COLS].rearrange("p (h d) -> p h d", h=GROUP_HEADS)
+            for i in range(GROUP_TILES):
+                tokens = slice(i * P, (i + 1) * P)
+                acc = acc_psum.tile([P, N_COLS], F32, name="acc")
+                for g in range(PASSES):
+                    nc.tensor.matmul_mx(
+                        out=acc[:],
+                        lhsT=x_codes[group][:, g, tokens].bitcast(FP8X4),
+                        lhsT_scale=x_scales[group][:, g, tokens],
+                        rhs=w_codes[c][:, g, :].bitcast(FP8X4),
+                        rhs_scale=w_scales[c][:, g, :],
+                        start=(g == 0),
+                        stop=(g == PASSES - 1),
+                    )
+                acc_heads = acc[:].rearrange("p (h d) -> p h d", h=GROUP_HEADS)
+                nc.vector.tensor_tensor(out=stage[:, :, i, :], in0=acc_heads, in1=bias_heads, op=ALU.add)
+            nc.sync.dma_start(
+                out=out_view[
+                    :,
+                    c * GROUP_HEADS : (c + 1) * GROUP_HEADS,
+                    group * GROUP_TILES : (group + 1) * GROUP_TILES,
+                    :,
+                ],
+                in_=stage[:],
+            )
+
+        xhat = {0: normalise(0)}
+        quantise_columns(0)
+        for step in range(COL_GROUPS):
+            if step < GROUPS:
+                quantise_tokens(step, xhat[step])
+            if step + 1 < GROUPS:
+                xhat[step + 1] = normalise(step + 1)
+            if step + 1 < COL_GROUPS:
+                quantise_columns(step + 1)
+            for group in range(min(step + 1, GROUPS)):
+                for c in range(step + 1):
+                    if max(group, c) == step:
+                        project(group, c)

@@ -166,7 +166,8 @@ def tile_localattentionblock_pa_kernel(
                 nc.scalar.activation(
                     out=xn[:, c, :], in_=xt[:], func=ACT.Identity, scale=gain[:, c // PACK, c % PACK : c % PACK + 1], bias=shift[:, c // PACK, c % PACK : c % PACK + 1]
                 )
-            grouped = [regroup(nc.vector.tensor_copy, xn[:, g * PACK : (g + 1) * PACK, :]) for g in range(PASSES)]
+            copy = nc.vector.tensor_copy if group == 0 else nc.scalar.copy
+            grouped = [regroup(copy, xn[:, g * PACK : (g + 1) * PACK, :]) for g in range(PASSES)]
             for g in range(PASSES):
                 quantise(grouped[g], x_codes[group][:, g, :], x_scales[group][:, g, :])
 

@@ -31,6 +31,7 @@ COL_GROUPS = COLS // N_COLS
 GROUP_HEADS = N_COLS // HEAD_DIM
 LOAD_COLS = 1024
 LOADS = COLS // LOAD_COLS
+LOAD_GROUPS = LOAD_COLS // N_COLS
 BN_WIDTH = 512
 BN_PARTS = DIM // BN_WIDTH
 BN_STATS = 6
@@ -50,10 +51,10 @@ def tile_localattentionblock_pa_kernel(
 
     with ExitStack() as ctx:
         keep = ctx.enter_context(tc.tile_pool(name="keep", bufs=1))
-        small = ctx.enter_context(tc.tile_pool(name="small", bufs=2 * GROUP_TILES))
+        small = ctx.enter_context(tc.tile_pool(name="small", bufs=TILES))
         xhat_pool = ctx.enter_context(tc.tile_pool(name="xhat_pool", bufs=2 * GROUP_TILES))
         xn_pool = ctx.enter_context(tc.tile_pool(name="xn_pool", bufs=2))
-        grouped_pool = ctx.enter_context(tc.tile_pool(name="grouped_pool", bufs=4))
+        grouped_pool = ctx.enter_context(tc.tile_pool(name="grouped_pool", bufs=3))
         stage_pool = ctx.enter_context(tc.tile_pool(name="stage_pool", bufs=4))
         xt_psum = ctx.enter_context(tc.psum_pool(name="xt_psum", bufs=4))
         acc_psum = ctx.enter_context(tc.psum_pool(name="acc_psum", bufs=4))
@@ -61,7 +62,7 @@ def tile_localattentionblock_pa_kernel(
         eps = keep.tile([P, 1], F32, name="eps")
         nc.vector.memset(eps[:], EPS)
         warm = keep.tile([P, 1], F32, name="warm")
-        nc.scalar.activation(out=warm[:], in_=eps[:], func=ACT.Sqrt)
+        nc.scalar.activation(out=warm[:], in_=eps[:], func=ACT.Abs_reciprocal_sqrt)
         ident = keep.tile([P, P], F32, name="ident")
         make_identity(nc, ident[:])
 
@@ -76,11 +77,8 @@ def tile_localattentionblock_pa_kernel(
             for t in range(group * GROUP_TILES, (group + 1) * GROUP_TILES):
                 nc.sync.dma_start(out=x_sb[t][:], in_=x_view[:, t, :])
 
-        def load_w(l):
-            for g in range(PASSES):
-                nc.sync.dma_start(
-                    out=w_raw[g][l][:], in_=w_view[g, :, :, l * LOAD_COLS : (l + 1) * LOAD_COLS]
-                )
+        def load_w(l, g):
+            nc.sync.dma_start(out=w_raw[g][l][:], in_=w_view[g, :, :, l * LOAD_COLS : (l + 1) * LOAD_COLS])
 
         vec_rows = keep.tile([P, K_PASS], BF16, name="vec_rows")
         nc.vector.memset(vec_rows[:], 0.0)
@@ -93,90 +91,102 @@ def tile_localattentionblock_pa_kernel(
         for v in range(len(vectors)):
             nc.scalar.dma_start(out=vec_rows[v * PASSES : (v + 1) * PASSES, :], in_=vectors[v])
         load_x(0)
-        load_w(0)
+        load_w(0, 0)
         load_x(1)
+        load_w(0, 1)
         load_x(2)
-        load_w(1)
         nc.sync.dma_start(out=bias[:], in_=qkv_b.partition_broadcast(P))
-        load_w(2)
-
-        vec_f32 = keep.tile([P, PACK, P], F32, name="vec_f32")
-        nc.vector.tensor_copy(out=vec_f32[:], in_=vec_rows[:].rearrange("r (q t) -> r t q", t=PACK))
-        vec_t = xt_psum.tile([P, GROUP_TOKENS], F32, name="xt")
-        for t in range(PACK):
-            nc.tensor.transpose(vec_t[:, t * P : (t + 1) * P], vec_f32[:, t, :], ident[:])
-        by_row = vec_t[:].rearrange("p (t r) -> p r t", t=PACK)
-        g_rows, b_rows, scale_rows, shift_rows = [by_row[:, v * PASSES : (v + 1) * PASSES, :] for v in range(len(vectors))]
-        one_plus = keep.tile([P, PASSES, PACK], F32, name="one_plus")
-        gain = keep.tile([P, PASSES, PACK], F32, name="gain")
-        shift = keep.tile([P, PASSES, PACK], F32, name="shift")
-        nc.vector.tensor_scalar_add(out=one_plus[:], in0=scale_rows, scalar1=1.0)
-        nc.vector.tensor_tensor(out=gain[:], in0=g_rows, in1=one_plus[:], op=ALU.mult)
-        nc.vector.tensor_tensor(out=shift[:], in0=b_rows, in1=one_plus[:], op=ALU.mult)
-        nc.vector.tensor_tensor(out=shift[:], in0=shift_rows, in1=shift[:], op=ALU.add)
+        for l in range(1, LOADS):
+            for g in range(PASSES):
+                load_w(l, g)
 
         x_codes = [keep.tile([P, PASSES, GROUP_TOKENS], U32, name="x_codes%d" % g, align_bytes=64) for g in range(GROUPS)]
         x_scales = [keep.tile([P, PASSES, GROUP_TOKENS], U8, name="x_scales%d" % g, align_bytes=64) for g in range(GROUPS)]
         w_codes = [keep.tile([P, PASSES, N_COLS], U32, name="w_codes%d" % c, align_bytes=64) for c in range(COL_GROUPS)]
         w_scales = [keep.tile([P, PASSES, N_COLS], U8, name="w_scales%d" % c, align_bytes=64) for c in range(COL_GROUPS)]
 
-        def regroup(copy, rows):
-            grouped = grouped_pool.tile([P, N_COLS, PACK], BF16, name="grouped", align_bytes=64)
+        gain = keep.tile([P, PASSES, PACK], F32, name="gain")
+        shift = keep.tile([P, PASSES, PACK], F32, name="shift")
+        xhat = {}
+        xn = {}
+        x_grouped = {}
+        w_grouped = {}
+
+        def modulation():
+            vec_f32 = keep.tile([P, PACK, P], F32, name="vec_f32")
+            nc.scalar.copy(out=vec_f32[:], in_=vec_rows[:].rearrange("r (q t) -> r t q", t=PACK))
+            vec_t = xt_psum.tile([P, GROUP_TOKENS], F32, name="xt")
+            for t in range(PACK):
+                nc.tensor.transpose(vec_t[:, t * P : (t + 1) * P], vec_f32[:, t, :], ident[:])
+            by_row = vec_t[:].rearrange("p (t r) -> p r t", t=PACK)
+            g_rows, b_rows, scale_rows, shift_rows = [
+                by_row[:, v * PASSES : (v + 1) * PASSES, :] for v in range(len(vectors))
+            ]
+            one_plus = keep.tile([P, PASSES, PACK], F32, name="one_plus")
+            nc.vector.tensor_scalar_add(out=one_plus[:], in0=scale_rows, scalar1=1.0)
+            nc.vector.tensor_tensor(out=gain[:], in0=g_rows, in1=one_plus[:], op=ALU.mult)
+            nc.vector.tensor_tensor(out=shift[:], in0=b_rows, in1=one_plus[:], op=ALU.mult)
+            nc.vector.tensor_tensor(out=shift[:], in0=shift_rows, in1=shift[:], op=ALU.add)
+
+        def normalise(t):
+            stats = small.tile([P, BN_PARTS, BN_STATS], F32, name="stats")
+            for h in range(BN_PARTS):
+                nc.vector.bn_stats(out=stats[:, h, :], in_=x_sb[t][:, h * BN_WIDTH : (h + 1) * BN_WIDTH])
+            mean_var = small.tile([P, 2], F32, name="mean_var")
+            nc.vector.bn_aggr(out=mean_var[:], in_=stats[:].rearrange("p h s -> p (h s)"))
+            neg_mean = small.tile([P, 1], F32, name="neg_mean")
+            nc.scalar.mul(out=neg_mean[:], in_=mean_var[:, 0:1], mul=-1.0)
+            rstd = small.tile([P, 1], F32, name="rstd")
+            nc.scalar.activation(out=rstd[:], in_=mean_var[:, 1:2], func=ACT.Abs_reciprocal_sqrt, bias=eps[:], scale=1.0)
+            xhat[t] = xhat_pool.tile([P, DIM], F32, name="xhat")
+            nc.gpsimd.tensor_scalar(
+                out=xhat[t][:].rearrange("p (g t q) -> p g t q", g=PASSES, t=PACK),
+                in0=x_sb[t][:].rearrange("p (g q t) -> p g t q", g=PASSES, t=PACK),
+                scalar1=neg_mean[:], scalar2=rstd[:],
+                op0=ALU.add, op1=ALU.mult,
+            )
+
+        def modulate(group, g):
+            xn[group, g] = xn_pool.tile([P, PACK, GROUP_TOKENS], BF16, name="xn%d" % g)
+            for t in range(PACK):
+                c = g * PACK + t
+                xt = xt_psum.tile([P, GROUP_TOKENS], F32, name="xt")
+                for i in range(GROUP_TILES):
+                    nc.tensor.transpose(
+                        xt[:, i * P : (i + 1) * P], xhat[group * GROUP_TILES + i][:, c * P : (c + 1) * P], ident[:]
+                    )
+                nc.scalar.activation(
+                    out=xn[group, g][:, t, :], in_=xt[:], func=ACT.Identity,
+                    scale=gain[:, g, t : t + 1], bias=shift[:, g, t : t + 1],
+                )
+
+        def regroup(copy, rows, name):
+            grouped = grouped_pool.tile([P, N_COLS, PACK], BF16, name=name, align_bytes=64)
             copy(
                 out=grouped[:].rearrange("p (c i) t -> p c t i", i=RUN),
                 in_=rows.rearrange("p t (c i) -> p c t i", i=RUN),
             )
             return grouped
 
+        def regroup_x(copy, group, g):
+            x_grouped[group, g] = regroup(copy, xn[group, g][:], "x_grouped")
+
+        def regroup_w(copy, c, g):
+            first = c % LOAD_GROUPS * N_COLS
+            w_grouped[c, g] = regroup(copy, w_raw[g][c // LOAD_GROUPS][:, :, first : first + N_COLS], "w_grouped")
+
         def quantise(grouped, codes, scales):
             nc.vector.quantize_mx(
                 out=codes.bitcast(FP8X4), scales=scales, in_=grouped[:].rearrange("p n t -> p (n t)")
             )
 
-        def normalise(group):
-            xhat = []
-            for t in range(group * GROUP_TILES, (group + 1) * GROUP_TILES):
-                stats = small.tile([P, BN_PARTS, BN_STATS], F32, name="stats")
-                for h in range(BN_PARTS):
-                    nc.vector.bn_stats(out=stats[:, h, :], in_=x_sb[t][:, h * BN_WIDTH : (h + 1) * BN_WIDTH])
-                mean_var = small.tile([P, 2], F32, name="mean_var")
-                nc.vector.bn_aggr(out=mean_var[:], in_=stats[:].rearrange("p h s -> p (h s)"))
-                neg_mean = small.tile([P, 1], F32, name="neg_mean")
-                nc.scalar.mul(out=neg_mean[:], in_=mean_var[:, 0:1], mul=-1.0)
-                std = small.tile([P, 1], F32, name="std")
-                nc.scalar.activation(out=std[:], in_=mean_var[:, 1:2], func=ACT.Sqrt, bias=eps[:], scale=1.0)
-                rstd = small.tile([P, 1], F32, name="rstd")
-                nc.vector.reciprocal(out=rstd[:], in_=std[:])
-                xhat_t = xhat_pool.tile([P, DIM], F32, name="xhat")
-                nc.gpsimd.tensor_scalar(
-                    out=xhat_t[:].rearrange("p (g t q) -> p g t q", g=PASSES, t=PACK),
-                    in0=x_sb[t][:].rearrange("p (g q t) -> p g t q", g=PASSES, t=PACK),
-                    scalar1=neg_mean[:], scalar2=rstd[:],
-                    op0=ALU.add, op1=ALU.mult,
-                )
-                xhat.append(xhat_t)
-            return xhat
-
-        def quantise_tokens(group, xhat):
-            xn = xn_pool.tile([P, K_CHUNKS, GROUP_TOKENS], BF16, name="xn")
-            for c in range(K_CHUNKS):
-                xt = xt_psum.tile([P, GROUP_TOKENS], F32, name="xt")
-                for i in range(GROUP_TILES):
-                    nc.tensor.transpose(xt[:, i * P : (i + 1) * P], xhat[i][:, c * P : (c + 1) * P], ident[:])
-                nc.scalar.activation(
-                    out=xn[:, c, :], in_=xt[:], func=ACT.Identity, scale=gain[:, c // PACK, c % PACK : c % PACK + 1], bias=shift[:, c // PACK, c % PACK : c % PACK + 1]
-                )
-            copy = nc.vector.tensor_copy if group == 0 else nc.scalar.copy
-            grouped = [regroup(copy, xn[:, g * PACK : (g + 1) * PACK, :]) for g in range(PASSES)]
+        def quantise_x(group):
             for g in range(PASSES):
-                quantise(grouped[g], x_codes[group][:, g, :], x_scales[group][:, g, :])
+                quantise(x_grouped[group, g], x_codes[group][:, g, :], x_scales[group][:, g, :])
 
-        def quantise_columns(c):
-            l = c * N_COLS // LOAD_COLS
-            first = c * N_COLS - l * LOAD_COLS
-            grouped = [regroup(nc.scalar.copy, w_raw[g][l][:, :, first : first + N_COLS]) for g in range(PASSES)]
+        def quantise_w(c):
             for g in range(PASSES):
-                quantise(grouped[g], w_codes[c][:, g, :], w_scales[c][:, g, :])
+                quantise(w_grouped[c, g], w_codes[c][:, g, :], w_scales[c][:, g, :])
 
         def project(group, c):
             stage = stage_pool.tile([P, GROUP_HEADS, GROUP_TILES, HEAD_DIM], F32, name="stage")
@@ -206,16 +216,58 @@ def tile_localattentionblock_pa_kernel(
                 in_=stage[:],
             )
 
-        xhat = {0: normalise(0)}
-        quantise_columns(0)
-        for step in range(COL_GROUPS):
-            if step < GROUPS:
-                quantise_tokens(step, xhat[step])
-            if step + 1 < GROUPS:
-                xhat[step + 1] = normalise(step + 1)
-            if step + 1 < COL_GROUPS:
-                quantise_columns(step + 1)
-            for group in range(min(step + 1, GROUPS)):
-                for c in range(step + 1):
-                    if max(group, c) == step:
-                        project(group, c)
+        vector_copy, scalar_copy = nc.vector.tensor_copy, nc.scalar.copy
+        normalise(0)
+        normalise(1)
+        regroup_w(scalar_copy, 0, 0)
+        normalise(2)
+        normalise(3)
+        modulation()
+        regroup_w(scalar_copy, 0, 1)
+        normalise(4)
+        normalise(5)
+        modulate(0, 0)
+        normalise(6)
+        normalise(7)
+        quantise_w(0)
+        modulate(0, 1)
+        regroup_x(vector_copy, 0, 0)
+        normalise(8)
+        regroup_x(vector_copy, 0, 1)
+        quantise_x(0)
+        regroup_w(scalar_copy, 1, 0)
+        regroup_w(scalar_copy, 1, 1)
+        normalise(9)
+        normalise(10)
+        normalise(11)
+        project(0, 0)
+        modulate(1, 0)
+        modulate(1, 1)
+        quantise_w(1)
+        project(0, 1)
+        regroup_x(vector_copy, 1, 0)
+        regroup_x(vector_copy, 1, 1)
+        regroup_w(scalar_copy, 2, 0)
+        regroup_w(scalar_copy, 2, 1)
+        quantise_x(1)
+        project(1, 0)
+        project(1, 1)
+        modulate(2, 0)
+        modulate(2, 1)
+        quantise_w(2)
+        project(0, 2)
+        project(1, 2)
+        regroup_x(scalar_copy, 2, 0)
+        regroup_x(scalar_copy, 2, 1)
+        quantise_x(2)
+        regroup_w(scalar_copy, 3, 0)
+        regroup_w(scalar_copy, 3, 1)
+        for c in range(3):
+            project(2, c)
+        for c in range(3, COL_GROUPS):
+            quantise_w(c)
+            if c + 1 < COL_GROUPS:
+                regroup_w(scalar_copy, c + 1, 0)
+                regroup_w(scalar_copy, c + 1, 1)
+            for group in range(GROUPS):
+                project(group, c)

@@ -35,6 +35,7 @@ LOAD_GROUPS = LOAD_COLS // N_COLS
 BN_WIDTH = 512
 BN_PARTS = DIM // BN_WIDTH
 BN_STATS = 6
+W_PIECES = 2
 RUN = 4
 
 FLOPS = 2 * TOKENS * DIM * COLS
@@ -89,7 +90,7 @@ def tile_localattentionblock_pa_kernel(
             t_shift.rearrange("b (r c) -> (b r) c", c=K_PASS),
         ]
         for v in range(len(vectors)):
-            nc.scalar.dma_start(out=vec_rows[v * PASSES : (v + 1) * PASSES, :], in_=vectors[v])
+            nc.sync.dma_start(out=vec_rows[v * PASSES : (v + 1) * PASSES, :], in_=vectors[v])
         load_x(0)
         load_w(0, 0)
         load_x(1)
@@ -160,20 +161,22 @@ def tile_localattentionblock_pa_kernel(
                     scale=gain[:, g, t : t + 1], bias=shift[:, g, t : t + 1],
                 )
 
-        def regroup(copy, rows, name):
+        def regroup(copy, rows, name, pieces):
             grouped = grouped_pool.tile([P, N_COLS, PACK], BF16, name=name, align_bytes=64)
-            copy(
-                out=grouped[:].rearrange("p (c i) t -> p c t i", i=RUN),
-                in_=rows.rearrange("p t (c i) -> p c t i", i=RUN),
-            )
+            for j in range(pieces):
+                cols = slice(j * N_COLS // pieces, (j + 1) * N_COLS // pieces)
+                copy(
+                    out=grouped[:, cols, :].rearrange("p (c i) t -> p c t i", i=RUN),
+                    in_=rows[:, :, cols].rearrange("p t (c i) -> p c t i", i=RUN),
+                )
             return grouped
 
         def regroup_x(copy, group, g):
-            x_grouped[group, g] = regroup(copy, xn[group, g][:], "x_grouped")
+            x_grouped[group, g] = regroup(copy, xn[group, g][:], "x_grouped", 1)
 
         def regroup_w(copy, c, g):
             first = c % LOAD_GROUPS * N_COLS
-            w_grouped[c, g] = regroup(copy, w_raw[g][c // LOAD_GROUPS][:, :, first : first + N_COLS], "w_grouped")
+            w_grouped[c, g] = regroup(copy, w_raw[g][c // LOAD_GROUPS][:, :, first : first + N_COLS], "w_grouped", W_PIECES)
 
         def quantise(grouped, codes, scales):
             nc.vector.quantize_mx(

@@ -196,7 +196,10 @@ def tile_localattentionblock_pa_kernel(
             bias_heads = bias[:, c * N_COLS : (c + 1) * N_COLS].rearrange("p (h d) -> p h d", h=GROUP_HEADS)
             for i in range(GROUP_TILES):
                 tokens = slice(i * P, (i + 1) * P)
-                acc = acc_psum.tile([P, N_COLS], F32, name="acc")
+                if c >= GROUPS and i % 2 == 1:
+                    acc = xt_psum.tile([P, N_COLS], F32, name="xt")
+                else:
+                    acc = acc_psum.tile([P, N_COLS], F32, name="acc")
                 for g in range(PASSES):
                     nc.tensor.matmul_mx(
                         out=acc[:],

@@ -246,21 +246,21 @@ def tile_localattentionblock_pa_kernel(
         normalise(9)
         normalise(10)
         normalise(11)
+        quantise_w(1)
         project(0, 0)
         modulate(1, 0)
         modulate(1, 1)
-        quantise_w(1)
         project(0, 1)
         regroup_x(vector_copy, 1, 0)
         regroup_x(vector_copy, 1, 1)
         regroup_w(scalar_copy, 2, 0)
         regroup_w(scalar_copy, 2, 1)
         quantise_x(1)
+        quantise_w(2)
         project(1, 0)
         project(1, 1)
         modulate(2, 0)
         modulate(2, 1)
-        quantise_w(2)
         project(0, 2)
         project(1, 2)
         regroup_x(scalar_copy, 2, 0)
@@ -268,12 +268,22 @@ def tile_localattentionblock_pa_kernel(
         quantise_x(2)
         regroup_w(scalar_copy, 3, 0)
         regroup_w(scalar_copy, 3, 1)
-        for c in range(3):
-            project(2, c)
-        for c in range(3, COL_GROUPS):
-            quantise_w(c)
-            if c + 1 < COL_GROUPS:
-                regroup_w(scalar_copy, c + 1, 0)
-                regroup_w(scalar_copy, c + 1, 1)
-            for group in range(GROUPS):
-                project(group, c)
+        project(2, 0)
+        project(2, 1)
+        quantise_w(3)
+        project(2, 2)
+        regroup_w(scalar_copy, 4, 0)
+        regroup_w(scalar_copy, 4, 1)
+        project(0, 3)
+        project(1, 3)
+        quantise_w(4)
+        project(2, 3)
+        regroup_w(scalar_copy, 5, 0)
+        regroup_w(scalar_copy, 5, 1)
+        project(0, 4)
+        project(1, 4)
+        quantise_w(5)
+        project(2, 4)
+        project(0, 5)
+        project(1, 5)
+        project(2, 5)

@@ -66,13 +66,15 @@ def tile_localattentionblock_pa_kernel(
         nc.scalar.activation(out=warm[:], in_=eps[:], func=ACT.Abs_reciprocal_sqrt)
         ident = keep.tile([P, P], F32, name="ident")
         make_identity(nc, ident[:])
+        ident_bf16 = keep.tile([P, P], BF16, name="ident_bf16")
+        make_identity(nc, ident_bf16[:])
 
         x_sb = [keep.tile([P, DIM], BF16, name="x_sb%d" % t) for t in range(TILES)]
         w_raw = [
             [keep.tile([P, PACK, LOAD_COLS], BF16, name="w_raw%d_%d" % (g, l)) for l in range(LOADS)]
             for g in range(PASSES)
         ]
-        bias = keep.tile([P, COLS], BF16, name="bias")
+        bias = [keep.tile([P, N_COLS], BF16, name="bias%d" % c) for c in range(COL_GROUPS)]
 
         def load_x(group):
             for t in range(group * GROUP_TILES, (group + 1) * GROUP_TILES):
@@ -91,12 +93,15 @@ def tile_localattentionblock_pa_kernel(
         ]
         for v in range(len(vectors)):
             nc.sync.dma_start(out=vec_rows[v * PASSES : (v + 1) * PASSES, :], in_=vectors[v])
+        bias_row = len(vectors) * PASSES
+        nc.sync.dma_start(
+            out=vec_rows[bias_row : bias_row + COL_GROUPS, :], in_=qkv_b.rearrange("(c n) -> c n", n=N_COLS)
+        )
         load_x(0)
         load_w(0, 0)
         load_x(1)
         load_w(0, 1)
         load_x(2)
-        nc.sync.dma_start(out=bias[:], in_=qkv_b.partition_broadcast(P))
         for l in range(1, LOADS):
             for g in range(PASSES):
                 load_w(l, g)
@@ -128,6 +133,14 @@ def tile_localattentionblock_pa_kernel(
             nc.vector.tensor_tensor(out=gain[:], in0=g_rows, in1=one_plus[:], op=ALU.mult)
             nc.vector.tensor_tensor(out=shift[:], in0=b_rows, in1=one_plus[:], op=ALU.mult)
             nc.vector.tensor_tensor(out=shift[:], in0=shift_rows, in1=shift[:], op=ALU.add)
+
+        def spread_bias(c):
+            spread = xt_psum.tile([P, N_COLS], F32, name="xt")
+            row = bias_row + c
+            nc.tensor.matmul(
+                spread[:], lhsT=ident_bf16[:, row : row + 1].to_broadcast([P, P]), rhs=vec_rows[:], start=True, stop=True
+            )
+            nc.scalar.copy(out=bias[c][:], in_=spread[:])
 
         def normalise(t):
             stats = small.tile([P, BN_PARTS, BN_STATS], F32, name="stats")
@@ -193,7 +206,7 @@ def tile_localattentionblock_pa_kernel(
 
         def project(group, c):
             stage = stage_pool.tile([P, GROUP_HEADS, GROUP_TILES, HEAD_DIM], F32, name="stage")
-            bias_heads = bias[:, c * N_COLS : (c + 1) * N_COLS].rearrange("p (h d) -> p h d", h=GROUP_HEADS)
+            bias_heads = bias[c][:].rearrange("p (h d) -> p h d", h=GROUP_HEADS)
             for i in range(GROUP_TILES):
                 tokens = slice(i * P, (i + 1) * P)
                 if c >= GROUPS and i % 2 == 1:
@@ -230,6 +243,7 @@ def tile_localattentionblock_pa_kernel(
         normalise(3)
         modulation()
         regroup_w(scalar_copy, 0, 1)
+        spread_bias(0)
         normalise(4)
         normalise(5)
         modulate(0, 0)
@@ -243,6 +257,7 @@ def tile_localattentionblock_pa_kernel(
         quantise_x(0)
         regroup_w(scalar_copy, 1, 0)
         regroup_w(scalar_copy, 1, 1)
+        spread_bias(1)
         normalise(9)
         normalise(10)
         normalise(11)
@@ -255,6 +270,7 @@ def tile_localattentionblock_pa_kernel(
         regroup_x(vector_copy, 1, 1)
         regroup_w(scalar_copy, 2, 0)
         regroup_w(scalar_copy, 2, 1)
+        spread_bias(2)
         quantise_x(1)
         quantise_w(2)
         project(1, 0)
@@ -268,18 +284,21 @@ def tile_localattentionblock_pa_kernel(
         quantise_x(2)
         regroup_w(scalar_copy, 3, 0)
         regroup_w(scalar_copy, 3, 1)
+        spread_bias(3)
         project(2, 0)
         project(2, 1)
         quantise_w(3)
         project(2, 2)
         regroup_w(scalar_copy, 4, 0)
         regroup_w(scalar_copy, 4, 1)
+        spread_bias(4)
         project(0, 3)
         project(1, 3)
         quantise_w(4)
         project(2, 3)
         regroup_w(scalar_copy, 5, 0)
         regroup_w(scalar_copy, 5, 1)
+        spread_bias(5)
         project(0, 4)
         project(1, 4)
         quantise_w(5)

from contextlib import ExitStack

import concourse.mybir as mybir
from concourse.masks import make_identity

F32 = mybir.dt.float32
BF16 = mybir.dt.bfloat16
U32 = mybir.dt.uint32
U8 = mybir.dt.uint8
FP8X4 = mybir.dt.float8_e4m3fn_x4
ALU = mybir.AluOpType
ACT = mybir.ActivationFunctionType

P = 128
TOKENS = 1536
DIM = 1024
COLS = 3072
HEAD_DIM = 128
EPS = 1e-5

PACK = 4
K_PASS = P * PACK
PASSES = DIM // K_PASS
K_CHUNKS = DIM // P
TILES = TOKENS // P
GROUP_TILES = 4
GROUPS = TILES // GROUP_TILES
GROUP_TOKENS = GROUP_TILES * P
N_COLS = 512
COL_GROUPS = COLS // N_COLS
GROUP_HEADS = N_COLS // HEAD_DIM
LOAD_COLS = 1024
LOADS = COLS // LOAD_COLS
LOAD_GROUPS = LOAD_COLS // N_COLS
BN_WIDTH = 512
BN_PARTS = DIM // BN_WIDTH
BN_STATS = 6
W_PIECES = 2
RUN = 4

FLOPS = 2 * TOKENS * DIM * COLS


def tile_localattentionblock_pa_kernel(
    tc, x, t_scale, t_shift, ln1_g, ln1_b, qkv_w, qkv_b, out
):
    nc = tc.nc

    x_view = x.rearrange("b (p t) k -> p (b t) k", t=TILES)
    out_view = out.rearrange("j b h (p t) d -> p (j b h) t d", t=TILES)
    w_view = qkv_w.rearrange("(g p t) n -> g p t n", t=PACK, p=P)

    with ExitStack() as ctx:
        keep = ctx.enter_context(tc.tile_pool(name="keep", bufs=1))
        small = ctx.enter_context(tc.tile_pool(name="small", bufs=TILES))
        xhat_pool = ctx.enter_context(tc.tile_pool(name="xhat_pool", bufs=2 * GROUP_TILES))
        xn_pool = ctx.enter_context(tc.tile_pool(name="xn_pool", bufs=2))
        grouped_pool = ctx.enter_context(tc.tile_pool(name="grouped_pool", bufs=3))
        stage_pool = ctx.enter_context(tc.tile_pool(name="stage_pool", bufs=4))
        xt_psum = ctx.enter_context(tc.psum_pool(name="xt_psum", bufs=4))
        acc_psum = ctx.enter_context(tc.psum_pool(name="acc_psum", bufs=4))

        eps = keep.tile([P, 1], F32, name="eps")
        nc.vector.memset(eps[:], EPS)
        warm = keep.tile([P, 1], F32, name="warm")
        nc.scalar.activation(out=warm[:], in_=eps[:], func=ACT.Abs_reciprocal_sqrt)
        ident = keep.tile([P, P], F32, name="ident")
        make_identity(nc, ident[:])
        ident_bf16 = keep.tile([P, P], BF16, name="ident_bf16")
        make_identity(nc, ident_bf16[:])

        x_sb = [keep.tile([P, DIM], BF16, name="x_sb%d" % t) for t in range(TILES)]
        w_raw = [
            [keep.tile([P, PACK, LOAD_COLS], BF16, name="w_raw%d_%d" % (g, l)) for l in range(LOADS)]
            for g in range(PASSES)
        ]
        bias = [keep.tile([P, N_COLS], BF16, name="bias%d" % c) for c in range(COL_GROUPS)]

        def load_x(group):
            for t in range(group * GROUP_TILES, (group + 1) * GROUP_TILES):
                nc.sync.dma_start(out=x_sb[t][:], in_=x_view[:, t, :])

        def load_w(l, g):
            nc.sync.dma_start(out=w_raw[g][l][:], in_=w_view[g, :, :, l * LOAD_COLS : (l + 1) * LOAD_COLS])

        vec_rows = keep.tile([P, K_PASS], BF16, name="vec_rows")
        nc.vector.memset(vec_rows[:], 0.0)
        vectors = [
            ln1_g.rearrange("(r c) -> r c", c=K_PASS),
            ln1_b.rearrange("(r c) -> r c", c=K_PASS),
            t_scale.rearrange("b (r c) -> (b r) c", c=K_PASS),
            t_shift.rearrange("b (r c) -> (b r) c", c=K_PASS),
        ]
        for v in range(len(vectors)):
            nc.sync.dma_start(out=vec_rows[v * PASSES : (v + 1) * PASSES, :], in_=vectors[v])
        bias_row = len(vectors) * PASSES
        nc.sync.dma_start(
            out=vec_rows[bias_row : bias_row + COL_GROUPS, :], in_=qkv_b.rearrange("(c n) -> c n", n=N_COLS)
        )
        load_x(0)
        load_w(0, 0)
        load_x(1)
        load_w(0, 1)
        load_x(2)
        for l in range(1, LOADS):
            for g in range(PASSES):
                load_w(l, g)

        x_codes = [keep.tile([P, PASSES, GROUP_TOKENS], U32, name="x_codes%d" % g, align_bytes=64) for g in range(GROUPS)]
        x_scales = [keep.tile([P, PASSES, GROUP_TOKENS], U8, name="x_scales%d" % g, align_bytes=64) for g in range(GROUPS)]
        w_codes = [keep.tile([P, PASSES, N_COLS], U32, name="w_codes%d" % c, align_bytes=64) for c in range(COL_GROUPS)]
        w_scales = [keep.tile([P, PASSES, N_COLS], U8, name="w_scales%d" % c, align_bytes=64) for c in range(COL_GROUPS)]

        gain = keep.tile([P, PASSES, PACK], F32, name="gain")
        shift = keep.tile([P, PASSES, PACK], F32, name="shift")
        xhat = {}
        xn = {}
        x_grouped = {}
        w_grouped = {}

        def modulation():
            vec_f32 = keep.tile([P, PACK, P], F32, name="vec_f32")
            nc.scalar.copy(out=vec_f32[:], in_=vec_rows[:].rearrange("r (q t) -> r t q", t=PACK))
            vec_t = xt_psum.tile([P, GROUP_TOKENS], F32, name="xt")
            for t in range(PACK):
                nc.tensor.transpose(vec_t[:, t * P : (t + 1) * P], vec_f32[:, t, :], ident[:])
            by_row = vec_t[:].rearrange("p (t r) -> p r t", t=PACK)
            g_rows, b_rows, scale_rows, shift_rows = [
                by_row[:, v * PASSES : (v + 1) * PASSES, :] for v in range(len(vectors))
            ]
            one_plus = keep.tile([P, PASSES, PACK], F32, name="one_plus")
            nc.vector.tensor_scalar_add(out=one_plus[:], in0=scale_rows, scalar1=1.0)
            nc.vector.tensor_tensor(out=gain[:], in0=g_rows, in1=one_plus[:], op=ALU.mult)
            nc.vector.tensor_tensor(out=shift[:], in0=b_rows, in1=one_plus[:], op=ALU.mult)
            nc.vector.tensor_tensor(out=shift[:], in0=shift_rows, in1=shift[:], op=ALU.add)

        def spread_bias(c):
            spread = xt_psum.tile([P, N_COLS], F32, name="xt")
            row = bias_row + c
            nc.tensor.matmul(
                spread[:], lhsT=ident_bf16[:, row : row + 1].to_broadcast([P, P]), rhs=vec_rows[:], start=True, stop=True
            )
            nc.scalar.copy(out=bias[c][:], in_=spread[:])

        def normalise(t):
            stats = small.tile([P, BN_PARTS, BN_STATS], F32, name="stats")
            for h in range(BN_PARTS):
                nc.vector.bn_stats(out=stats[:, h, :], in_=x_sb[t][:, h * BN_WIDTH : (h + 1) * BN_WIDTH])
            mean_var = small.tile([P, 2], F32, name="mean_var")
            nc.vector.bn_aggr(out=mean_var[:], in_=stats[:].rearrange("p h s -> p (h s)"))
            neg_mean = small.tile([P, 1], F32, name="neg_mean")
            nc.scalar.mul(out=neg_mean[:], in_=mean_var[:, 0:1], mul=-1.0)
            rstd = small.tile([P, 1], F32, name="rstd")
            nc.scalar.activation(out=rstd[:], in_=mean_var[:, 1:2], func=ACT.Abs_reciprocal_sqrt, bias=eps[:], scale=1.0)
            xhat[t] = xhat_pool.tile([P, DIM], F32, name="xhat")
            nc.gpsimd.tensor_scalar(
                out=xhat[t][:].rearrange("p (g t q) -> p g t q", g=PASSES, t=PACK),
                in0=x_sb[t][:].rearrange("p (g q t) -> p g t q", g=PASSES, t=PACK),
                scalar1=neg_mean[:], scalar2=rstd[:],
                op0=ALU.add, op1=ALU.mult,
            )

        def modulate(group, g):
            xn[group, g] = xn_pool.tile([P, PACK, GROUP_TOKENS], BF16, name="xn%d" % g)
            for t in range(PACK):
                c = g * PACK + t
                xt = xt_psum.tile([P, GROUP_TOKENS], F32, name="xt")
                for i in range(GROUP_TILES):
                    nc.tensor.transpose(
                        xt[:, i * P : (i + 1) * P], xhat[group * GROUP_TILES + i][:, c * P : (c + 1) * P], ident[:]
                    )
                nc.scalar.activation(
                    out=xn[group, g][:, t, :], in_=xt[:], func=ACT.Identity,
                    scale=gain[:, g, t : t + 1], bias=shift[:, g, t : t + 1],
                )

        def regroup(copy, rows, name, pieces):
            grouped = grouped_pool.tile([P, N_COLS, PACK], BF16, name=name, align_bytes=64)
            for j in range(pieces):
                cols = slice(j * N_COLS // pieces, (j + 1) * N_COLS // pieces)
                copy(
                    out=grouped[:, cols, :].rearrange("p (c i) t -> p c t i", i=RUN),
                    in_=rows[:, :, cols].rearrange("p t (c i) -> p c t i", i=RUN),
                )
            return grouped

        def regroup_x(copy, group, g):
            x_grouped[group, g] = regroup(copy, xn[group, g][:], "x_grouped", 1)

        def regroup_w(copy, c, g):
            first = c % LOAD_GROUPS * N_COLS
            w_grouped[c, g] = regroup(copy, w_raw[g][c // LOAD_GROUPS][:, :, first : first + N_COLS], "w_grouped", W_PIECES)

        def quantise(grouped, codes, scales):
            nc.vector.quantize_mx(
                out=codes.bitcast(FP8X4), scales=scales, in_=grouped[:].rearrange("p n t -> p (n t)")
            )

        def quantise_x(group):
            for g in range(PASSES):
                quantise(x_grouped[group, g], x_codes[group][:, g, :], x_scales[group][:, g, :])

        def quantise_w(c):
            for g in range(PASSES):
                quantise(w_grouped[c, g], w_codes[c][:, g, :], w_scales[c][:, g, :])

        def project(group, c):
            stage = stage_pool.tile([P, GROUP_HEADS, GROUP_TILES, HEAD_DIM], F32, name="stage")
            bias_heads = bias[c][:].rearrange("p (h d) -> p h d", h=GROUP_HEADS)
            for i in range(GROUP_TILES):
                tokens = slice(i * P, (i + 1) * P)
                if c >= GROUPS and i % 2 == 1:
                    acc = xt_psum.tile([P, N_COLS], F32, name="xt")
                else:
                    acc = acc_psum.tile([P, N_COLS], F32, name="acc")
                for g in range(PASSES):
                    nc.tensor.matmul_mx(
                        out=acc[:],
                        lhsT=x_codes[group][:, g, tokens].bitcast(FP8X4),
                        lhsT_scale=x_scales[group][:, g, tokens],
                        rhs=w_codes[c][:, g, :].bitcast(FP8X4),
                        rhs_scale=w_scales[c][:, g, :],
                        start=(g == 0),
                        stop=(g == PASSES - 1),
                    )
                acc_heads = acc[:].rearrange("p (h d) -> p h d", h=GROUP_HEADS)
                nc.vector.tensor_tensor(out=stage[:, :, i, :], in0=acc_heads, in1=bias_heads, op=ALU.add)
            nc.sync.dma_start(
                out=out_view[
                    :,
                    c * GROUP_HEADS : (c + 1) * GROUP_HEADS,
                    group * GROUP_TILES : (group + 1) * GROUP_TILES,
                    :,
                ],
                in_=stage[:],
            )

        vector_copy, scalar_copy = nc.vector.tensor_copy, nc.scalar.copy
        normalise(0)
        normalise(1)
        regroup_w(scalar_copy, 0, 0)
        normalise(2)
        normalise(3)
        modulation()
        regroup_w(scalar_copy, 0, 1)
        spread_bias(0)
        normalise(4)
        normalise(5)
        modulate(0, 0)
        normalise(6)
        normalise(7)
        quantise_w(0)
        modulate(0, 1)
        regroup_x(vector_copy, 0, 0)
        normalise(8)
        regroup_x(vector_copy, 0, 1)
        quantise_x(0)
        regroup_w(scalar_copy, 1, 0)
        regroup_w(scalar_copy, 1, 1)
        spread_bias(1)
        normalise(9)
        normalise(10)
        normalise(11)
        quantise_w(1)
        project(0, 0)
        modulate(1, 0)
        modulate(1, 1)
        project(0, 1)
        regroup_x(vector_copy, 1, 0)
        regroup_x(vector_copy, 1, 1)
        regroup_w(scalar_copy, 2, 0)
        regroup_w(scalar_copy, 2, 1)
        spread_bias(2)
        quantise_x(1)
        quantise_w(2)
        project(1, 0)
        project(1, 1)
        modulate(2, 0)
        modulate(2, 1)
        project(0, 2)
        project(1, 2)
        regroup_x(scalar_copy, 2, 0)
        regroup_x(scalar_copy, 2, 1)
        quantise_x(2)
        regroup_w(scalar_copy, 3, 0)
        regroup_w(scalar_copy, 3, 1)
        spread_bias(3)
        project(2, 0)
        project(2, 1)
        quantise_w(3)
        project(2, 2)
        regroup_w(scalar_copy, 4, 0)
        regroup_w(scalar_copy, 4, 1)
        spread_bias(4)
        project(0, 3)
        project(1, 3)
        quantise_w(4)
        project(2, 3)
        regroup_w(scalar_copy, 5, 0)
        regroup_w(scalar_copy, 5, 1)
        spread_bias(5)
        project(0, 4)
        project(1, 4)
        quantise_w(5)
        project(2, 4)
        project(0, 5)
        project(1, 5)
        project(2, 5)
